import numpy as np
import ml_dtypes


def mxq(x, axis, fmt="e4m3"):
    dtype, down = {"e4m3": (ml_dtypes.float8_e4m3fn, 7), "e5m2": (ml_dtypes.float8_e5m2, 14)}[fmt]
    v = np.moveaxis(np.asarray(x, np.float32).astype(ml_dtypes.bfloat16).astype(np.float64), axis, -1)
    blocks = v.reshape(v.shape[:-1] + (-1, 32))
    amax = np.abs(blocks).max(-1, keepdims=True)
    byte = np.maximum(np.where(amax > 0, np.frexp(amax)[1] - 1 + 127, 0) - down, 1)
    scale = np.exp2(byte - 127.0)
    codes = (blocks / scale).astype(np.float32).astype(dtype).astype(np.float64)
    return np.moveaxis((codes * scale).reshape(v.shape), -1, axis)


WIDE = False


def mx_kscale(k):
    if not WIDE:
        return np.ones(k)
    levels = np.array([10, -10, 5, -5, 0])
    a = np.random.permutation(np.resize(levels, k // 512 * 4)).reshape(k // 512, 4)
    idx = np.arange(k)
    return np.exp2(a[idx // 512, idx % 128 // 32])


BF16 = ml_dtypes.bfloat16


def bf(x):
    return np.asarray(x, np.float32).astype(BF16)


def f64(x):
    return np.asarray(x).astype(np.float64)


B, L, F, D, N = 128, 32, 512, 1024, 8192
TOP = 0.8 * np.sqrt(2.0 * np.log(L))


def elu(v):
    return np.where(v > 0.0, v, np.exp(np.minimum(v, 0.0)) - 1.0)


def setup_inputs():
    s = mx_kscale(F)
    return {"x": bf(np.random.standard_normal((B, L, F)) * s),
            "conv_w": bf(np.random.standard_normal((D, F)) / np.sqrt(F) / s),
            "conv_b": bf(np.random.standard_normal(D) * 2.0 - TOP)}


def reference(x, conv_w, conv_b):
    z = (mxq(f64(x), 2, "e4m3") @ mxq(f64(conv_w), 1, "e4m3").T) + f64(conv_b)
    return elu(z).max(axis=1)

@@ -1,0 +1,162 @@
+from contextlib import ExitStack
+
+import concourse.mybir as mybir
+from concourse.masks import make_identity
+
+F32 = mybir.dt.float32
+BF16 = mybir.dt.bfloat16
+U32 = mybir.dt.uint32
+U8 = mybir.dt.uint8
+FP8X4 = mybir.dt.float8_e4m3fn_x4
+ALU = mybir.AluOpType
+ACT = mybir.ActivationFunctionType
+
+P = 128
+SEQS, POSITIONS, FEATURES, CHANNELS = 128, 32, 512, 1024
+WORDS = FEATURES // 2
+PAIR = 2
+PAIR_COLS = PAIR * P
+HALF = 512
+HALVES = CHANNELS // HALF
+GROUP = 4
+CHAINS = 2
+
+FLOPS = 2 * SEQS * POSITIONS * FEATURES * CHANNELS
+
+
+def tile_conceptembedmodel_pa_kernel(tc, x, conv_w, conv_b, out):
+    nc = tc.nc
+    with ExitStack() as ctx:
+        keep = ctx.enter_context(tc.tile_pool(name="keep", bufs=1))
+        stage = ctx.enter_context(tc.tile_pool(name="stage", bufs=4))
+        running = ctx.enter_context(tc.tile_pool(name="running", bufs=2))
+        finish_pool = ctx.enter_context(tc.tile_pool(name="finish", bufs=2))
+        turn_pool = ctx.enter_context(tc.psum_pool(name="turn", bufs=3))
+        z_pool = ctx.enter_context(tc.psum_pool(name="z", bufs=5))
+        ctx.enter_context(tc.manual_schedule())
+
+        ident = keep.tile([P, P], F32)
+        make_identity(nc, ident[:])
+
+        x_raw = keep.tile([P, POSITIONS * FEATURES], BF16)
+        w_raw = keep.tile([P, (CHANNELS // P) * FEATURES], BF16)
+        bias = keep.tile([P, CHANNELS], BF16)
+        raw_cols = PAIR * FEATURES
+
+        def load_w_pair(j):
+            nc.sync.dma_start(
+                out=w_raw[:, j * raw_cols : (j + 1) * raw_cols].rearrange(
+                    "r (s f) -> r s f", s=PAIR
+                ),
+                in_=conv_w[j * PAIR_COLS : (j + 1) * PAIR_COLS, :].rearrange(
+                    "(s r) f -> r s f", s=PAIR
+                ),
+            )
+
+        def load_x_pair(j):
+            nc.sync.dma_start(
+                out=x_raw[:, j * raw_cols : (j + 1) * raw_cols],
+                in_=x[:, j * PAIR : (j + 1) * PAIR, :].rearrange("b l f -> b (l f)"),
+            )
+
+        pairs_per_half = HALF // PAIR_COLS
+        for j in range(pairs_per_half):
+            load_w_pair(j)
+        for j in range(POSITIONS // PAIR):
+            load_x_pair(j)
+        for j in range(pairs_per_half, HALVES * pairs_per_half):
+            load_w_pair(j)
+        nc.sync.dma_start(out=bias[:], in_=conv_b.partition_broadcast(P))
+
+        x_codes = keep.tile([P, POSITIONS * P], U32, align_bytes=64)
+        x_scales = keep.tile([P, POSITIONS * P], U8, align_bytes=64)
+        w_codes = keep.tile([P, CHANNELS], U32, align_bytes=64)
+        w_scales = keep.tile([P, CHANNELS], U8, align_bytes=64)
+        x_words = x_raw[:].bitcast(F32)
+        w_words = w_raw[:].bitcast(F32)
+
+        def prepare_pair(words, codes, scales, j):
+            turned = turn_pool.tile([P, PAIR, 2, P], F32)
+            for s in range(PAIR):
+                for u in range(2):
+                    first = (j * PAIR + s) * WORDS + u * P
+                    nc.tensor.transpose(turned[:, s, u, :], words[:, first : first + P], ident[:])
+            grouped = stage.tile([P, PAIR_COLS * 4], BF16, align_bytes=64)
+            nc.scalar.copy(
+                out=grouped[:].bitcast(F32).rearrange("p (s r u) -> p s r u", s=PAIR, u=2),
+                in_=turned[:].rearrange("p s u r -> p s r u"),
+            )
+            cols = slice(j * PAIR_COLS, (j + 1) * PAIR_COLS)
+            nc.vector.quantize_mx(
+                out=codes[:, cols].bitcast(FP8X4), scales=scales[:, cols], in_=grouped[:]
+            )
+
+        def prepare_x_group(g):
+            for j in range(g * GROUP // PAIR, (g + 1) * GROUP // PAIR):
+                prepare_pair(x_words, x_codes, x_scales, j)
+
+        def prepare_w_half(h):
+            for j in range(h * pairs_per_half, (h + 1) * pairs_per_half):
+                prepare_pair(w_words, w_codes, w_scales, j)
+
+        def new_maxima():
+            return [running.tile([P, HALF], F32, name="best%d" % c) for c in range(CHAINS)]
+
+        def multiply_and_fold(h, l, best):
+            z = z_pool.tile([P, HALF], F32)
+            seqs = slice(l * P, (l + 1) * P)
+            chans = slice(h * HALF, (h + 1) * HALF)
+            nc.tensor.matmul_mx(
+                out=z[:],
+                lhsT=x_codes[:, seqs].bitcast(FP8X4),
+                lhsT_scale=x_scales[:, seqs],
+                rhs=w_codes[:, chans].bitcast(FP8X4),
+                rhs_scale=w_scales[:, chans],
+                start=True,
+                stop=True,
+            )
+            chain = best[l % CHAINS]
+            if l < CHAINS:
+                nc.scalar.copy(out=chain[:], in_=z[:])
+            else:
+                nc.vector.tensor_tensor(out=chain[:], in0=z[:], in1=chain[:], op=ALU.max)
+
+        def finish_half(h, best, engine):
+            chans = slice(h * HALF, (h + 1) * HALF)
+            top = finish_pool.tile([P, HALF], F32)
+            nc.vector.tensor_tensor(out=top[:], in0=best[0][:], in1=best[1][:], op=ALU.max)
+            v = finish_pool.tile([P, HALF], F32)
+            engine.tensor_tensor(out=v[:], in0=top[:], in1=bias[:, chans], op=ALU.add)
+            below = finish_pool.tile([P, HALF], F32)
+            engine.tensor_scalar(out=below[:], in0=v[:], scalar1=0.0, scalar2=None, op0=ALU.min)
+            grown = finish_pool.tile([P, HALF], F32)
+            nc.scalar.activation(out=grown[:], in_=below[:], func=ACT.Exp)
+            above = finish_pool.tile([P, HALF], F32)
+            engine.tensor_scalar(
+                out=above[:], in0=v[:], scalar1=0.0, scalar2=-1.0, op0=ALU.max, op1=ALU.add
+            )
+            result = finish_pool.tile([P, HALF], F32)
+            engine.tensor_tensor(out=result[:], in0=above[:], in1=grown[:], op=ALU.add)
+            nc.sync.dma_start(out=out[:, chans], in_=result[:])
+
+        prepare_w_half(0)
+        prepare_x_group(0)
+        groups = POSITIONS // GROUP
+        best_first = new_maxima()
+        for g in range(groups):
+            for l in range(g * GROUP, g * GROUP + GROUP // 2):
+                multiply_and_fold(0, l, best_first)
+            if g + 1 < groups:
+                prepare_x_group(g + 1)
+            else:
+                prepare_w_half(1)
+            for l in range(g * GROUP + GROUP // 2, (g + 1) * GROUP):
+                multiply_and_fold(0, l, best_first)
+
+        best_second = new_maxima()
+        for l in range(CHAINS):
+            multiply_and_fold(1, l, best_second)
+        finish_half(0, best_first, nc.gpsimd)
+        for l in range(CHAINS, POSITIONS):
+            multiply_and_fold(1, l, best_second)
+        finish_half(1, best_second, nc.vector)

@@ -7,6 +7,7 @@ F32 = mybir.dt.float32
 BF16 = mybir.dt.bfloat16
 U32 = mybir.dt.uint32
 U8 = mybir.dt.uint8
+I32 = mybir.dt.int32
 FP8X4 = mybir.dt.float8_e4m3fn_x4
 ALU = mybir.AluOpType
 ACT = mybir.ActivationFunctionType
@@ -18,7 +19,9 @@ PAIR = 2
 PAIR_COLS = PAIR * P
 HALF = 512
 HALVES = CHANNELS // HALF
-GROUP = 4
+AHEAD = 2
+WARM_UP = 6
+PIECES = 2
 CHAINS = 2
 
 FLOPS = 2 * SEQS * POSITIONS * FEATURES * CHANNELS
@@ -28,7 +31,7 @@ def tile_conceptembedmodel_pa_kernel(tc, x, conv_w, conv_b, out):
     nc = tc.nc
     with ExitStack() as ctx:
         keep = ctx.enter_context(tc.tile_pool(name="keep", bufs=1))
-        stage = ctx.enter_context(tc.tile_pool(name="stage", bufs=4))
+        stage = ctx.enter_context(tc.tile_pool(name="stage", bufs=AHEAD + 2))
         running = ctx.enter_context(tc.tile_pool(name="running", bufs=2))
         finish_pool = ctx.enter_context(tc.tile_pool(name="finish", bufs=2))
         turn_pool = ctx.enter_context(tc.psum_pool(name="turn", bufs=3))
@@ -37,6 +40,16 @@ def tile_conceptembedmodel_pa_kernel(tc, x, conv_w, conv_b, out):
 
         ident = keep.tile([P, P], F32)
         make_identity(nc, ident[:])
+
+        zeros = keep.tile([P, HALF], BF16)
+        nc.vector.memset(zeros[:].bitcast(I32), 0)
+
+        def idle_matmul():
+            unread = z_pool.tile([P, HALF], F32, tag="z")
+            nc.tensor.matmul(out=unread[:], lhsT=zeros[:, :P], rhs=zeros[:], start=True, stop=True)
+
+        for i in range(WARM_UP):
+            idle_matmul()
 
         x_raw = keep.tile([P, POSITIONS * FEATURES], BF16)
         w_raw = keep.tile([P, (CHANNELS // P) * FEATURES], BF16)
@@ -75,7 +88,7 @@ def tile_conceptembedmodel_pa_kernel(tc, x, conv_w, conv_b, out):
         x_words = x_raw[:].bitcast(F32)
         w_words = w_raw[:].bitcast(F32)
 
-        def prepare_pair(words, codes, scales, j):
+        def turn_pair(words, j):
             turned = turn_pool.tile([P, PAIR, 2, P], F32)
             for s in range(PAIR):
                 for u in range(2):
@@ -86,18 +99,13 @@ def tile_conceptembedmodel_pa_kernel(tc, x, conv_w, conv_b, out):
                 out=grouped[:].bitcast(F32).rearrange("p (s r u) -> p s r u", s=PAIR, u=2),
                 in_=turned[:].rearrange("p s u r -> p s r u"),
             )
+            return grouped
+
+        def quantise_pair(grouped, codes, scales, j):
             cols = slice(j * PAIR_COLS, (j + 1) * PAIR_COLS)
             nc.vector.quantize_mx(
                 out=codes[:, cols].bitcast(FP8X4), scales=scales[:, cols], in_=grouped[:]
             )
-
-        def prepare_x_group(g):
-            for j in range(g * GROUP // PAIR, (g + 1) * GROUP // PAIR):
-                prepare_pair(x_words, x_codes, x_scales, j)
-
-        def prepare_w_half(h):
-            for j in range(h * pairs_per_half, (h + 1) * pairs_per_half):
-                prepare_pair(w_words, w_codes, w_scales, j)
 
         def new_maxima():
             return [running.tile([P, HALF], F32, name="best%d" % c) for c in range(CHAINS)]
@@ -128,30 +136,45 @@ def tile_conceptembedmodel_pa_kernel(tc, x, conv_w, conv_b, out):
             v = finish_pool.tile([P, HALF], F32)
             engine.tensor_tensor(out=v[:], in0=top[:], in1=bias[:, chans], op=ALU.add)
             below = finish_pool.tile([P, HALF], F32)
-            engine.tensor_scalar(out=below[:], in0=v[:], scalar1=0.0, scalar2=None, op0=ALU.min)
             grown = finish_pool.tile([P, HALF], F32)
-            nc.scalar.activation(out=grown[:], in_=below[:], func=ACT.Exp)
             above = finish_pool.tile([P, HALF], F32)
+            result = finish_pool.tile([P, HALF], F32)
+            width = HALF // PIECES
+            pieces = [slice(c * width, (c + 1) * width) for c in range(PIECES)]
+            for piece in pieces:
+                engine.tensor_scalar(
+                    out=below[:, piece], in0=v[:, piece], scalar1=0.0, scalar2=None, op0=ALU.min
+                )
+                nc.scalar.activation(out=grown[:, piece], in_=below[:, piece], func=ACT.Exp)
             engine.tensor_scalar(
                 out=above[:], in0=v[:], scalar1=0.0, scalar2=-1.0, op0=ALU.max, op1=ALU.add
             )
-            result = finish_pool.tile([P, HALF], F32)
-            engine.tensor_tensor(out=result[:], in0=above[:], in1=grown[:], op=ALU.add)
-            nc.sync.dma_start(out=out[:, chans], in_=result[:])
+            for c in range(PIECES):
+                piece = pieces[c]
+                engine.tensor_tensor(
+                    out=result[:, piece], in0=above[:, piece], in1=grown[:, piece], op=ALU.add
+                )
+                first = h * HALF + c * width
+                nc.sync.dma_start(out=out[:, first : first + width], in_=result[:, piece])
 
-        prepare_w_half(0)
-        prepare_x_group(0)
-        groups = POSITIONS // GROUP
+        x_pairs = POSITIONS // PAIR
+        to_prepare = [(w_words, w_codes, w_scales, j) for j in range(pairs_per_half)]
+        to_prepare += [(x_words, x_codes, x_scales, j) for j in range(x_pairs)]
+        to_prepare += [
+            (w_words, w_codes, w_scales, j) for j in range(pairs_per_half, HALVES * pairs_per_half)
+        ]
+        started = pairs_per_half + AHEAD
+        for words, codes, scales, i in to_prepare[:started]:
+            quantise_pair(turn_pair(words, i), codes, scales, i)
+            idle_matmul()
         best_first = new_maxima()
-        for g in range(groups):
-            for l in range(g * GROUP, g * GROUP + GROUP // 2):
+        for j in range(x_pairs):
+            coming = to_prepare[started + j : started + j + 1]
+            regrouped = [turn_pair(words, i) for words, codes, scales, i in coming]
+            for l in range(j * PAIR, (j + 1) * PAIR):
                 multiply_and_fold(0, l, best_first)
-            if g + 1 < groups:
-                prepare_x_group(g + 1)
-            else:
-                prepare_w_half(1)
-            for l in range(g * GROUP + GROUP // 2, (g + 1) * GROUP):
-                multiply_and_fold(0, l, best_first)
+            for grouped, (words, codes, scales, i) in zip(regrouped, coming):
+                quantise_pair(grouped, codes, scales, i)
 
         best_second = new_maxima()
         for l in range(CHAINS):

@@ -7,7 +7,6 @@ F32 = mybir.dt.float32
 BF16 = mybir.dt.bfloat16
 U32 = mybir.dt.uint32
 U8 = mybir.dt.uint8
-I32 = mybir.dt.int32
 FP8X4 = mybir.dt.float8_e4m3fn_x4
 ALU = mybir.AluOpType
 ACT = mybir.ActivationFunctionType
@@ -20,7 +19,6 @@ PAIR_COLS = PAIR * P
 HALF = 512
 HALVES = CHANNELS // HALF
 AHEAD = 2
-WARM_UP = 6
 PIECES = 2
 CHAINS = 2
 
@@ -40,16 +38,6 @@ def tile_conceptembedmodel_pa_kernel(tc, x, conv_w, conv_b, out):
 
         ident = keep.tile([P, P], F32)
         make_identity(nc, ident[:])
-
-        zeros = keep.tile([P, HALF], BF16)
-        nc.vector.memset(zeros[:].bitcast(I32), 0)
-
-        def idle_matmul():
-            unread = z_pool.tile([P, HALF], F32, tag="z")
-            nc.tensor.matmul(out=unread[:], lhsT=zeros[:, :P], rhs=zeros[:], start=True, stop=True)
-
-        for i in range(WARM_UP):
-            idle_matmul()
 
         x_raw = keep.tile([P, POSITIONS * FEATURES], BF16)
         w_raw = keep.tile([P, (CHANNELS // P) * FEATURES], BF16)
@@ -166,7 +154,6 @@ def tile_conceptembedmodel_pa_kernel(tc, x, conv_w, conv_b, out):
         started = pairs_per_half + AHEAD
         for words, codes, scales, i in to_prepare[:started]:
             quantise_pair(turn_pair(words, i), codes, scales, i)
-            idle_matmul()
         best_first = new_maxima()
         for j in range(x_pairs):
             coming = to_prepare[started + j : started + j + 1]

from contextlib import ExitStack

import concourse.mybir as mybir
from concourse.masks import make_identity

F32 = mybir.dt.float32
BF16 = mybir.dt.bfloat16
U32 = mybir.dt.uint32
U8 = mybir.dt.uint8
FP8X4 = mybir.dt.float8_e4m3fn_x4
ALU = mybir.AluOpType
ACT = mybir.ActivationFunctionType

P = 128
SEQS, POSITIONS, FEATURES, CHANNELS = 128, 32, 512, 1024
WORDS = FEATURES // 2
PAIR = 2
PAIR_COLS = PAIR * P
HALF = 512
HALVES = CHANNELS // HALF
AHEAD = 2
PIECES = 2
CHAINS = 2

FLOPS = 2 * SEQS * POSITIONS * FEATURES * CHANNELS


def tile_conceptembedmodel_pa_kernel(tc, x, conv_w, conv_b, out):
    nc = tc.nc
    with ExitStack() as ctx:
        keep = ctx.enter_context(tc.tile_pool(name="keep", bufs=1))
        stage = ctx.enter_context(tc.tile_pool(name="stage", bufs=AHEAD + 2))
        running = ctx.enter_context(tc.tile_pool(name="running", bufs=2))
        finish_pool = ctx.enter_context(tc.tile_pool(name="finish", bufs=2))
        turn_pool = ctx.enter_context(tc.psum_pool(name="turn", bufs=3))
        z_pool = ctx.enter_context(tc.psum_pool(name="z", bufs=5))
        ctx.enter_context(tc.manual_schedule())

        ident = keep.tile([P, P], F32)
        make_identity(nc, ident[:])

        x_raw = keep.tile([P, POSITIONS * FEATURES], BF16)
        w_raw = keep.tile([P, (CHANNELS // P) * FEATURES], BF16)
        bias = keep.tile([P, CHANNELS], BF16)
        raw_cols = PAIR * FEATURES

        def load_w_pair(j):
            nc.sync.dma_start(
                out=w_raw[:, j * raw_cols : (j + 1) * raw_cols].rearrange(
                    "r (s f) -> r s f", s=PAIR
                ),
                in_=conv_w[j * PAIR_COLS : (j + 1) * PAIR_COLS, :].rearrange(
                    "(s r) f -> r s f", s=PAIR
                ),
            )

        def load_x_pair(j):
            nc.sync.dma_start(
                out=x_raw[:, j * raw_cols : (j + 1) * raw_cols],
                in_=x[:, j * PAIR : (j + 1) * PAIR, :].rearrange("b l f -> b (l f)"),
            )

        pairs_per_half = HALF // PAIR_COLS
        for j in range(pairs_per_half):
            load_w_pair(j)
        for j in range(POSITIONS // PAIR):
            load_x_pair(j)
        for j in range(pairs_per_half, HALVES * pairs_per_half):
            load_w_pair(j)
        nc.sync.dma_start(out=bias[:], in_=conv_b.partition_broadcast(P))

        x_codes = keep.tile([P, POSITIONS * P], U32, align_bytes=64)
        x_scales = keep.tile([P, POSITIONS * P], U8, align_bytes=64)
        w_codes = keep.tile([P, CHANNELS], U32, align_bytes=64)
        w_scales = keep.tile([P, CHANNELS], U8, align_bytes=64)
        x_words = x_raw[:].bitcast(F32)
        w_words = w_raw[:].bitcast(F32)

        def turn_pair(words, j):
            turned = turn_pool.tile([P, PAIR, 2, P], F32)
            for s in range(PAIR):
                for u in range(2):
                    first = (j * PAIR + s) * WORDS + u * P
                    nc.tensor.transpose(turned[:, s, u, :], words[:, first : first + P], ident[:])
            grouped = stage.tile([P, PAIR_COLS * 4], BF16, align_bytes=64)
            nc.scalar.copy(
                out=grouped[:].bitcast(F32).rearrange("p (s r u) -> p s r u", s=PAIR, u=2),
                in_=turned[:].rearrange("p s u r -> p s r u"),
            )
            return grouped

        def quantise_pair(grouped, codes, scales, j):
            cols = slice(j * PAIR_COLS, (j + 1) * PAIR_COLS)
            nc.vector.quantize_mx(
                out=codes[:, cols].bitcast(FP8X4), scales=scales[:, cols], in_=grouped[:]
            )

        def new_maxima():
            return [running.tile([P, HALF], F32, name="best%d" % c) for c in range(CHAINS)]

        def multiply_and_fold(h, l, best):
            z = z_pool.tile([P, HALF], F32)
            seqs = slice(l * P, (l + 1) * P)
            chans = slice(h * HALF, (h + 1) * HALF)
            nc.tensor.matmul_mx(
                out=z[:],
                lhsT=x_codes[:, seqs].bitcast(FP8X4),
                lhsT_scale=x_scales[:, seqs],
                rhs=w_codes[:, chans].bitcast(FP8X4),
                rhs_scale=w_scales[:, chans],
                start=True,
                stop=True,
            )
            chain = best[l % CHAINS]
            if l < CHAINS:
                nc.scalar.copy(out=chain[:], in_=z[:])
            else:
                nc.vector.tensor_tensor(out=chain[:], in0=z[:], in1=chain[:], op=ALU.max)

        def finish_half(h, best, engine):
            chans = slice(h * HALF, (h + 1) * HALF)
            top = finish_pool.tile([P, HALF], F32)
            nc.vector.tensor_tensor(out=top[:], in0=best[0][:], in1=best[1][:], op=ALU.max)
            v = finish_pool.tile([P, HALF], F32)
            engine.tensor_tensor(out=v[:], in0=top[:], in1=bias[:, chans], op=ALU.add)
            below = finish_pool.tile([P, HALF], F32)
            grown = finish_pool.tile([P, HALF], F32)
            above = finish_pool.tile([P, HALF], F32)
            result = finish_pool.tile([P, HALF], F32)
            width = HALF // PIECES
            pieces = [slice(c * width, (c + 1) * width) for c in range(PIECES)]
            for piece in pieces:
                engine.tensor_scalar(
                    out=below[:, piece], in0=v[:, piece], scalar1=0.0, scalar2=None, op0=ALU.min
                )
                nc.scalar.activation(out=grown[:, piece], in_=below[:, piece], func=ACT.Exp)
            engine.tensor_scalar(
                out=above[:], in0=v[:], scalar1=0.0, scalar2=-1.0, op0=ALU.max, op1=ALU.add
            )
            for c in range(PIECES):
                piece = pieces[c]
                engine.tensor_tensor(
                    out=result[:, piece], in0=above[:, piece], in1=grown[:, piece], op=ALU.add
                )
                first = h * HALF + c * width
                nc.sync.dma_start(out=out[:, first : first + width], in_=result[:, piece])

        x_pairs = POSITIONS // PAIR
        to_prepare = [(w_words, w_codes, w_scales, j) for j in range(pairs_per_half)]
        to_prepare += [(x_words, x_codes, x_scales, j) for j in range(x_pairs)]
        to_prepare += [
            (w_words, w_codes, w_scales, j) for j in range(pairs_per_half, HALVES * pairs_per_half)
        ]
        started = pairs_per_half + AHEAD
        for words, codes, scales, i in to_prepare[:started]:
            quantise_pair(turn_pair(words, i), codes, scales, i)
        best_first = new_maxima()
        for j in range(x_pairs):
            coming = to_prepare[started + j : started + j + 1]
            regrouped = [turn_pair(words, i) for words, codes, scales, i in coming]
            for l in range(j * PAIR, (j + 1) * PAIR):
                multiply_and_fold(0, l, best_first)
            for grouped, (words, codes, scales, i) in zip(regrouped, coming):
                quantise_pair(grouped, codes, scales, i)

        best_second = new_maxima()
        for l in range(CHAINS):
            multiply_and_fold(1, l, best_second)
        finish_half(0, best_first, nc.gpsimd)
        for l in range(CHAINS, POSITIONS):
            multiply_and_fold(1, l, best_second)
        finish_half(1, best_second, nc.vector)
